import numpy as np
import ml_dtypes


def mxq(x, axis, fmt="e4m3"):
    dtype, down = {"e4m3": (ml_dtypes.float8_e4m3fn, 7), "e5m2": (ml_dtypes.float8_e5m2, 14)}[fmt]
    v = np.moveaxis(np.asarray(x, np.float32).astype(ml_dtypes.bfloat16).astype(np.float64), axis, -1)
    blocks = v.reshape(v.shape[:-1] + (-1, 32))
    amax = np.abs(blocks).max(-1, keepdims=True)
    byte = np.maximum(np.where(amax > 0, np.frexp(amax)[1] - 1 + 127, 0) - down, 1)
    scale = np.exp2(byte - 127.0)
    codes = (blocks / scale).astype(np.float32).astype(dtype).astype(np.float64)
    return np.moveaxis((codes * scale).reshape(v.shape), -1, axis)


WIDE = False


def mx_kscale(k):
    if not WIDE:
        return np.ones(k)
    levels = np.array([10, -10, 5, -5, 0])
    if k % 512:
        return np.exp2(np.random.permutation(np.resize(levels, k // 32))).repeat(32)
    a = np.empty((k // 512, 16))
    for p in range(k // 512):
        a[p, :8] = np.random.permutation(np.resize(levels, 8))
        for g in range(8):
            far = levels[np.abs(levels - a[p, g]) >= 10]
            a[p, g + 8] = far[np.random.randint(len(far))]
    return np.exp2(a.ravel()).repeat(32)


BF16 = ml_dtypes.bfloat16


def bf(x):
    return np.asarray(x, np.float32).astype(BF16)


def f64(x):
    return np.asarray(x).astype(np.float64)


N, A, B, C = 256, 2048, 64, 32


def setup_inputs():
    s = mx_kscale(A)
    return {"x": bf(np.random.standard_normal((N, A)) * s),
            "T": bf(np.random.standard_normal((A, B, C)) * 3.2 / (C * np.sqrt(A)) / s[:, None, None])}


def reference(x, T):
    Afeat, Bout, Crow = T.shape
    Ms = (mxq(f64(x), 1, "e4m3") @ mxq(f64(T).reshape(Afeat, Bout * Crow), 0, "e4m3")).reshape(-1, Bout, Crow)
    l1 = np.stack([np.abs(Ms[i][None, :, :] - Ms).sum(axis=-1) for i in range(Ms.shape[0])])
    return np.exp(-l1).sum(axis=1)

@@ -1,0 +1,368 @@
+from contextlib import ExitStack
+
+import concourse.mybir as mybir
+from concourse.masks import make_identity
+
+FP8X4 = mybir.dt.float8_e4m3fn_x4
+F32 = mybir.dt.float32
+BF16 = mybir.dt.bfloat16
+U32 = mybir.dt.uint32
+U8 = mybir.dt.uint8
+ALU = mybir.AluOpType
+ACT = mybir.ActivationFunctionType
+
+N = 256
+A = 2048
+B = 64
+C = 32
+P = 128
+BC = B * C
+FLOPS = 2 * N * A * BC + 3 * N * N * BC
+
+NPE = 55
+NGP = 12
+LAG = 4
+
+
+def tile_minibatchdiscrimination_kernel(tc, x, T, out):
+    nc = tc.nc
+    odd = [ii for ii in range(P) if ii % 2 == 1]
+    skip = [odd[(k + 1) * 64 // (64 - NPE) - 1] for k in range(64 - NPE)]
+    PEROWS = [ii for ii in odd if ii not in skip]
+    rest = [ii for ii in range(P) if ii not in PEROWS]
+    GROWS = [rest[(k * len(rest)) // NGP] for k in range(NGP)]
+    FROWS = [ii for ii in rest if ii not in GROWS]
+    NPR = len(PEROWS)
+    NFR = len(FROWS)
+    PEBANK = [PEROWS[4 * k:4 * k + 4] for k in range((NPR + 3) // 4)]
+    nblk = (NFR + 3) // 4
+    FBLK = [list(range(k * NFR // nblk, (k + 1) * NFR // nblk)) for k in range(nblk)]
+    with ExitStack() as ctx:
+        ctx.enter_context(tc.manual_schedule())
+        const = ctx.enter_context(tc.tile_pool(name="const", bufs=1))
+        psum = ctx.enter_context(tc.psum_pool(name="psum", bufs=1))
+
+        def bank(i, shape, nm):
+            return psum.tile(shape, F32, tag="bank%d" % i, name=nm)
+
+        ident = const.tile([P, P], F32, name="ident")
+        make_identity(nc, ident[:])
+        zt = const.tile([P, P], F32, name="zt")
+        nc.vector.memset(zt[:], 0.0)
+        colv = const.tile([P, 4, 256], F32, name="colv")
+        nc.vector.memset(colv[:], 0.0)
+        onesm = const.tile([P, 1], F32, name="onesm")
+        mt = const.tile([P, C, 256], F32, name="mt")
+        nhr = const.tile([P, 256], F32, name="nhr")
+        rsb = const.tile([P, P], F32, name="rsb")
+        nrs = const.tile([P, P], F32, name="nrs")
+        u3 = const.tile([P, C, 3, B], F32, name="u3")
+        ownf = const.tile([P, P], F32, name="ownf")
+        planes = {}
+        nc.vector.memset(ownf[:], 0.0)
+        w = const.tile([P, 256], F32, name="w")
+        z1 = const.tile([P, P], F32, name="z1")
+        res = const.tile([P, 2, B], F32, name="res")
+
+        with ExitStack() as mxs:
+            keep = mxs.enter_context(tc.tile_pool(name="keep", bufs=1))
+            rawp = mxs.enter_context(tc.tile_pool(name="rawp", bufs=4))
+            grpp = mxs.enter_context(tc.tile_pool(name="grpp", bufs=4))
+            cdp = mxs.enter_context(tc.tile_pool(name="cdp", bufs=4))
+
+            xsb = []
+            for m in range(2):
+                xm = keep.tile([P, A], BF16, name="xsb%d" % m)
+                nc.sync.dma_start(out=xm[:], in_=x[m * P:(m + 1) * P, :])
+                xsb.append(xm)
+            tv = T.rearrange("(g q j) b c -> g q j (b c)", g=4, q=P, j=4)
+            raws = []
+            for g in range(4):
+                raw = rawp.tile([P, 4, BC], BF16, name="raw")
+                for u in range(2):
+                    nc.sync.dma_start(
+                        out=raw[:, :, 1024 * u:1024 * (u + 1)],
+                        in_=tv[g, :, :, 1024 * u:1024 * (u + 1)],
+                    )
+                raws.append(raw)
+
+            nc.vector.tensor_scalar(out=onesm[:], in0=ident[:, P - 1:P], scalar1=-1.0, scalar2=1.0,
+                                    op0=ALU.mult, op1=ALU.add)
+
+            gx = keep.tile([P, 4, 1024], BF16, name="gx", align_bytes=64)
+            xq = keep.tile([P, 4, N], U32, name="xq", align_bytes=64)
+            xs = keep.tile([P, 4, N], U8, name="xs", align_bytes=64)
+            xts = []
+            for g in range(4):
+                xt = bank(g, [P, 2, N], "xt")
+                for m in range(2):
+                    for u in range(2):
+                        nc.tensor.transpose(xt[:, u, m * P:(m + 1) * P],
+                                            xsb[m][:].bitcast(F32)[:, 256 * g + u:256 * (g + 1):2], ident[:])
+                xts.append(xt)
+            for g in range(4):
+                dst = gx[:, g, :].bitcast(F32).rearrange("p (i u) -> p i u", u=2)
+                src = xts[g][:].rearrange("p u i -> p i u")
+                if g % 2 == 0:
+                    nc.vector.tensor_copy(out=dst, in_=src)
+                else:
+                    nc.scalar.copy(out=dst, in_=src)
+            for g in range(4):
+                nc.vector.quantize_mx(out=xq[:, g, :].bitcast(FP8X4), scales=xs[:, g, :], in_=gx[:, g, :])
+
+            acc = [[None] * 4, [None] * 4]
+            grps = {}
+
+            def regroup(j):
+                g, nt = j // 4, j % 4
+                grp = grpp.tile([P, 512, 4], BF16, name="grp", align_bytes=64)
+                dst = grp[:].rearrange("p (c i) t -> p c t i", i=4)
+                src = raws[g][:, :, nt * 512:(nt + 1) * 512].rearrange("p t (c i) -> p c t i", i=4)
+                if j % 2 == 0:
+                    nc.vector.tensor_copy(out=dst, in_=src)
+                else:
+                    nc.scalar.copy(out=dst, in_=src)
+                grps[j] = grp
+
+            def quant_mm(j):
+                g, nt = j // 4, j % 4
+                tq = cdp.tile([P, 512], U32, name="tq", align_bytes=64)
+                ts = cdp.tile([P, 512], U8, name="ts", align_bytes=64)
+                nc.vector.quantize_mx(out=tq[:].bitcast(FP8X4), scales=ts[:],
+                                      in_=grps[j][:].rearrange("p n t -> p (n t)"))
+                for m in range(2):
+                    if g == 0:
+                        acc[m][nt] = bank(4 * m + nt, [P, 512], "acc")
+                    nc.tensor.matmul_mx(
+                        out=acc[m][nt][:],
+                        lhsT=xq[:, g, m * P:(m + 1) * P].bitcast(FP8X4),
+                        lhsT_scale=xs[:, g, m * P:(m + 1) * P],
+                        rhs=tq[:].bitcast(FP8X4),
+                        rhs_scale=ts[:],
+                        start=(g == 0),
+                        stop=(g == 3),
+                    )
+
+            regroup(0)
+            regroup(1)
+            for pr in range(8):
+                if pr < 7:
+                    regroup(2 * pr + 2)
+                    regroup(2 * pr + 3)
+                quant_mm(2 * pr)
+                quant_mm(2 * pr + 1)
+
+
+            def evac(m, nt, s, eng):
+                dst = u3[:, :, s, 16 * nt:16 * nt + 16]
+                src = acc[m][nt][:].rearrange("p (b c) -> p c b", c=C)
+                if eng == 0:
+                    nc.vector.tensor_copy(out=dst, in_=src)
+                else:
+                    nc.scalar.copy(out=dst, in_=src)
+
+            for nt in range(3):
+                evac(0, nt, 0, 0)
+                evac(0, nt, 2, 0)
+            evac(0, 3, 0, 1)
+            evac(0, 3, 2, 1)
+            for nt in range(4):
+                evac(1, nt, 1, 1)
+
+            r3 = keep.tile([P, 3, B], F32, name="r3")
+            nc.vector.tensor_reduce(out=r3[:, 0:2, :], in_=u3[:, :, 0:2, :].rearrange("p c s b -> p s b c"),
+                                    axis=mybir.AxisListType.X, op=ALU.add)
+            nc.vector.tensor_copy(out=r3[:, 2, :], in_=r3[:, 0, :])
+
+            rps = bank(6, [P, 2, P], "rps")
+            for cp in range(C // 2):
+                mtp = bank(4 + cp if cp < 2 else cp % 4, [P, 2, 256], "mtp")
+                if cp < 2:
+                    planes[cp] = mtp
+                for cc in range(2):
+                    c = 2 * cp + cc
+                    flat = u3[:, c, :, :].rearrange("p s b -> p (s b)")
+                    for u in range(2):
+                        nc.tensor.transpose(mtp[:, cc, u * P:(u + 1) * P], flat[:, u * B:u * B + P], ident[:])
+                nc.scalar.copy(out=mt[:, 2 * cp:2 * cp + 2, :], in_=mtp[:])
+                if cp == 11:
+                    rflat = r3[:].rearrange("p s b -> p (s b)")
+                    for u in range(2):
+                        nc.tensor.transpose(rps[:, u, :], rflat[:, u * B:u * B + P], ident[:])
+                    nc.vector.tensor_scalar(out=nhr[:], in0=rps[:].rearrange("p u k -> p (u k)"), scalar1=-0.5,
+                                            scalar2=None, op0=ALU.mult)
+                    nc.vector.tensor_copy(out=rsb[:], in_=rps[:, 0, :])
+                    nc.vector.tensor_scalar(out=nrs[:], in0=rps[:, 0, :], scalar1=-1.0, scalar2=None, op0=ALU.mult)
+
+        aspool = ctx.enter_context(tc.tile_pool(name="aspool", bufs=5))
+        work = ctx.enter_context(tc.tile_pool(name="work", bufs=4))
+        big = ctx.enter_context(tc.tile_pool(name="big", bufs=1))
+
+        colps = bank(6, [P, 256], "colps")
+        ownps = bank(7, [P, P], "ownps")
+
+        def load_planes(rho):
+            pl = bank(4 + rho % 2, [P, 2, 256], "pl")
+            for cc in range(2):
+                flat = u3[:, 2 * rho + cc, :, :].rearrange("p s b -> p (s b)")
+                for u in range(2):
+                    nc.tensor.transpose(pl[:, cc, u * P:(u + 1) * P], flat[:, u * B:u * B + P], ident[:])
+            planes[rho] = pl
+
+        nc.tensor.matmul(out=colps[:, 0:P], lhsT=zt[:], rhs=ident[:], is_transpose=True, start=True, stop=False)
+        nc.tensor.matmul(out=colps[:, P:2 * P], lhsT=zt[:], rhs=ident[:], is_transpose=True, start=False,
+                         stop=False)
+        nc.tensor.matmul(out=ownps[:], lhsT=zt[:], rhs=ident[:], is_transpose=True, start=True, stop=True)
+
+        gbs = [big.tile([P, C, P], F32, name="gb0"), big.tile([P, C, P], F32, name="gb1")]
+        gacc = big.tile([P, NGP, P], F32, name="gacc")
+        for g2 in range(0, NGP, 2):
+            pair = [gi for gi in (g2, g2 + 1) if gi < NGP]
+            for gi in pair:
+                ii = GROWS[gi]
+                nc.gpsimd.tensor_tensor(out=gbs[gi % 2][:], in0=mt[:, :, ii + 1:ii + 1 + P],
+                                        in1=mt[:, :, ii:ii + 1].to_broadcast([P, C, P]), op=ALU.subtract)
+            for gi in pair:
+                nc.gpsimd.tensor_scalar(out=gbs[gi % 2][:], in0=gbs[gi % 2][:], scalar1=3.0e38, scalar2=0.0,
+                                        op0=ALU.min, op1=ALU.max)
+            for wd in (16, 8, 4, 2, 1):
+                for gi in pair:
+                    gb = gbs[gi % 2]
+                    nc.gpsimd.tensor_tensor(out=gb[:, 0:wd, :], in0=gb[:, 0:wd, :], in1=gb[:, wd:2 * wd, :],
+                                            op=ALU.add)
+            for gi in pair:
+                ii = GROWS[gi]
+                nc.gpsimd.tensor_tensor(out=gacc[:, gi, :], in0=gbs[gi % 2][:, 0, :],
+                                        in1=nhr[:, ii + 1:ii + 1 + P], op=ALU.add)
+
+        accall = big.tile([P, NFR, P], F32, name="accall")
+        l1s = {}
+        ess = {}
+        ncol = [0]
+
+        def col_add(ii, src):
+            k = ncol[0] % 4
+            ncol[0] += 1
+            nc.vector.tensor_tensor(out=colv[:, k, ii + 1:ii + P], in0=colv[:, k, ii + 1:ii + P], in1=src,
+                                    op=ALU.add)
+
+        def fused_step(fi, c):
+            ii = FROWS[fi]
+            pl = planes[c // 2]
+            prev = nhr[:, ii + 1:ii + 1 + P] if c == 0 else accall[:, fi, :]
+            nc.vector.scalar_tensor_tensor(out=accall[:, fi, :], in0=pl[:, c % 2, ii + 1:ii + 1 + P],
+                                           scalar=pl[:, c % 2, ii:ii + 1], in1=prev, op0=ALU.max, op1=ALU.add)
+
+        def fused_exp(k):
+            for fi in FBLK[k]:
+                ii = FROWS[fi]
+                nc.scalar.activation(out=accall[:, fi, :], in_=accall[:, fi, :], func=ACT.Exp, scale=-2.0,
+                                     bias=rsb[:, ii:ii + 1], accum_out=ownf[:, ii:ii + 1])
+
+        def fused_cols(k):
+            for fi in FBLK[k]:
+                col_add(FROWS[fi], accall[:, fi, 0:P - 1])
+
+        def gp_exp():
+            for gi in range(NGP):
+                ii = GROWS[gi]
+                nc.scalar.activation(out=gacc[:, gi, :], in_=gacc[:, gi, :], func=ACT.Exp, scale=-2.0,
+                                     bias=nrs[:, ii:ii + 1], accum_out=ownf[:, ii:ii + 1])
+
+        def gp_cols():
+            for gi in range(NGP):
+                col_add(GROWS[gi], gacc[:, gi, 0:P - 1])
+
+        def bank_exp(b):
+            ess[b] = work.tile([P, 4, P], F32, name="es4")
+            nr = len(PEBANK[b])
+            nc.scalar.activation(out=ess[b][:, 0:nr, :], in_=l1s[b][:, 0:nr, :], func=ACT.Exp, scale=-1.0)
+
+        def bank_sums(b):
+            for r in range(len(PEBANK[b])):
+                ii = PEBANK[b][r]
+                nc.tensor.matmul(out=colps[:, ii + 1:ii + 1 + P], lhsT=ess[b][:, r, :], rhs=ident[:],
+                                 is_transpose=True, start=False, stop=(4 * b + r == NPR - 1))
+                nc.tensor.matmul(out=ownps[:, ii:ii + 1], lhsT=ess[b][:, r, :], rhs=onesm[:],
+                                 start=True, stop=True)
+
+        steps = []
+        for rho in range(C // 2):
+            for blk in FBLK:
+                for cc in range(2):
+                    for fi in blk:
+                        steps.append((fi, 2 * rho + cc))
+        nstt = len(steps)
+
+        def slot_of(i):
+            return ((i + 1) * NPR + nstt - 1) // nstt - 1
+
+        ev_s = {}
+        ev_pe = {}
+        ev_v = {}
+
+        def at(table, slot, what):
+            table[slot] = table.get(slot, []) + [what]
+
+        for b in range(len(PEBANK)):
+            es_slot = min(4 * b + 3 + LAG, NPR if b == len(PEBANK) - 1 else NPR - 1)
+            at(ev_s, es_slot, (0, b))
+            at(ev_pe, es_slot + 1, (0, b))
+        for rho in range(2, C // 2):
+            at(ev_pe, slot_of(int((rho - 0.6) * 2 * NFR)), (1, rho))
+        at(ev_s, NPR - 2, (2, 0))
+        at(ev_v, NPR + 2, (2, 0))
+        done = (C // 2 - 1) * 2 * NFR
+        for k in range(nblk):
+            done += 2 * len(FBLK[k])
+            at(ev_s, slot_of(done - 1) + 1, (1, k))
+            at(ev_v, max(slot_of(done - 1) + 2, NPR), (1, k))
+
+        for slot in range(NPR + 3):
+            if slot < NPR:
+                for i in range(slot * nstt // NPR, (slot + 1) * nstt // NPR):
+                    fused_step(steps[i][0], steps[i][1])
+            for kind, k in ev_v.get(slot, []):
+                if kind == 1:
+                    fused_cols(k)
+                else:
+                    gp_cols()
+            if slot < NPR:
+                ii = PEROWS[slot]
+                b = slot // 4
+                r = slot % 4
+                if r == 0:
+                    l1s[b] = bank(b % 4, [P, 4, P], "l1t")
+                pas = aspool.tile([P, C, P], F32, name="pas")
+                for c in range(C):
+                    nc.scalar.activation(out=pas[:, c, :], in_=mt[:, c, ii + 1:ii + 1 + P], func=ACT.Abs,
+                                         scale=-1.0, bias=mt[:, c, ii:ii + 1])
+                    nc.tensor.matmul(out=l1s[b][:, r, :], lhsT=pas[:, c, :], rhs=ident[:], is_transpose=True,
+                                     start=(c == 0), stop=(c == C - 1))
+            for kind, k in ev_pe.get(slot, []):
+                if kind == 0:
+                    bank_sums(k)
+                else:
+                    load_planes(k)
+            for kind, k in sorted(ev_s.get(slot, []), key=lambda e: (e[0] == 0, e[0], e[1])):
+                if kind == 0:
+                    bank_exp(k)
+                elif kind == 1:
+                    fused_exp(k)
+                else:
+                    gp_exp()
+
+        nc.vector.tensor_tensor(out=w[:], in0=colv[:, 0, :], in1=colps[:], op=ALU.add)
+        nc.vector.tensor_tensor(out=colv[:, 1, :], in0=colv[:, 1, :], in1=colv[:, 2, :], op=ALU.add)
+        nc.vector.tensor_tensor(out=colv[:, 3, 0:P], in0=colv[:, 3, 0:P], in1=ownps[:], op=ALU.add)
+        nc.vector.tensor_tensor(out=w[:, 0:P], in0=w[:, 0:P], in1=ownf[:], op=ALU.add)
+        nc.vector.tensor_tensor(out=colv[:, 1, :], in0=colv[:, 1, :], in1=colv[:, 3, :], op=ALU.add)
+        nc.vector.tensor_tensor(out=w[:], in0=w[:], in1=colv[:, 1, :], op=ALU.add)
+        zps = bank(0, [P, 2, P], "zps")
+        for u in range(2):
+            nc.tensor.transpose(zps[:, u, :], w[:, u * P:(u + 1) * P], ident[:])
+        nc.vector.tensor_copy(out=z1[:], in_=zps[:, 1, :])
+        for h in range(2):
+            nc.vector.scalar_tensor_tensor(out=res[:, h, :], in0=zps[:, 0, h * B:(h + 1) * B], scalar=1.0,
+                                           in1=z1[:, (1 - h) * B:(2 - h) * B], op0=ALU.add, op1=ALU.add)
+        nc.sync.dma_start(out=out.rearrange("(h t) b -> t h b", h=2), in_=res[:])

@@ -19,22 +19,23 @@ P = 128
 BC = B * C
 FLOPS = 2 * N * A * BC + 3 * N * N * BC
 
-NPE = 55
-NGP = 12
-LAG = 4
+NSC = 48
+NGP = 26
+LAG = 2
 
 
 def tile_minibatchdiscrimination_kernel(tc, x, T, out):
     nc = tc.nc
-    odd = [ii for ii in range(P) if ii % 2 == 1]
-    skip = [odd[(k + 1) * 64 // (64 - NPE) - 1] for k in range(64 - NPE)]
-    PEROWS = [ii for ii in odd if ii not in skip]
-    rest = [ii for ii in range(P) if ii not in PEROWS]
-    GROWS = [rest[(k * len(rest)) // NGP] for k in range(NGP)]
-    FROWS = [ii for ii in rest if ii not in GROWS]
-    NPR = len(PEROWS)
+    quota = [NSC, NGP, P - NSC - NGP]
+    owner = []
+    for i in range(P):
+        owner.append(max(range(3), key=lambda o: quota[o] * (i + 1) - P * sum(1 for w in owner if w == o)))
+    SROWS = [i for i in range(P) if owner[i] == 0]
+    GROWS = [i for i in range(P) if owner[i] == 1]
+    FROWS = [i for i in range(P) if owner[i] == 2]
     NFR = len(FROWS)
-    PEBANK = [PEROWS[4 * k:4 * k + 4] for k in range((NPR + 3) // 4)]
+    SBANK = [SROWS[4 * k:4 * k + 4] for k in range((NSC + 3) // 4)]
+    GBANK = [GROWS[4 * k:4 * k + 4] for k in range((NGP + 3) // 4)]
     nblk = (NFR + 3) // 4
     FBLK = [list(range(k * NFR // nblk, (k + 1) * NFR // nblk)) for k in range(nblk)]
     with ExitStack() as ctx:
@@ -55,7 +56,6 @@ def tile_minibatchdiscrimination_kernel(tc, x, T, out):
         mt = const.tile([P, C, 256], F32, name="mt")
         nhr = const.tile([P, 256], F32, name="nhr")
         rsb = const.tile([P, P], F32, name="rsb")
-        nrs = const.tile([P, P], F32, name="nrs")
         u3 = const.tile([P, C, 3, B], F32, name="u3")
         ownf = const.tile([P, P], F32, name="ownf")
         planes = {}
@@ -192,9 +192,9 @@ def tile_minibatchdiscrimination_kernel(tc, x, T, out):
                     nc.vector.tensor_scalar(out=nhr[:], in0=rps[:].rearrange("p u k -> p (u k)"), scalar1=-0.5,
                                             scalar2=None, op0=ALU.mult)
                     nc.vector.tensor_copy(out=rsb[:], in_=rps[:, 0, :])
-                    nc.vector.tensor_scalar(out=nrs[:], in0=rps[:, 0, :], scalar1=-1.0, scalar2=None, op0=ALU.mult)
 
-        aspool = ctx.enter_context(tc.tile_pool(name="aspool", bufs=5))
+        aspool = ctx.enter_context(tc.tile_pool(name="aspool", bufs=4))
+        gpool = ctx.enter_context(tc.tile_pool(name="gpool", bufs=3))
         work = ctx.enter_context(tc.tile_pool(name="work", bufs=4))
         big = ctx.enter_context(tc.tile_pool(name="big", bufs=1))
 
@@ -214,31 +214,21 @@ def tile_minibatchdiscrimination_kernel(tc, x, T, out):
                          stop=False)
         nc.tensor.matmul(out=ownps[:], lhsT=zt[:], rhs=ident[:], is_transpose=True, start=True, stop=True)
 
-        gbs = [big.tile([P, C, P], F32, name="gb0"), big.tile([P, C, P], F32, name="gb1")]
-        gacc = big.tile([P, NGP, P], F32, name="gacc")
-        for g2 in range(0, NGP, 2):
-            pair = [gi for gi in (g2, g2 + 1) if gi < NGP]
-            for gi in pair:
-                ii = GROWS[gi]
-                nc.gpsimd.tensor_tensor(out=gbs[gi % 2][:], in0=mt[:, :, ii + 1:ii + 1 + P],
-                                        in1=mt[:, :, ii:ii + 1].to_broadcast([P, C, P]), op=ALU.subtract)
-            for gi in pair:
-                nc.gpsimd.tensor_scalar(out=gbs[gi % 2][:], in0=gbs[gi % 2][:], scalar1=3.0e38, scalar2=0.0,
-                                        op0=ALU.min, op1=ALU.max)
-            for wd in (16, 8, 4, 2, 1):
-                for gi in pair:
-                    gb = gbs[gi % 2]
-                    nc.gpsimd.tensor_tensor(out=gb[:, 0:wd, :], in0=gb[:, 0:wd, :], in1=gb[:, wd:2 * wd, :],
-                                            op=ALU.add)
-            for gi in pair:
-                ii = GROWS[gi]
-                nc.gpsimd.tensor_tensor(out=gacc[:, gi, :], in0=gbs[gi % 2][:, 0, :],
-                                        in1=nhr[:, ii + 1:ii + 1 + P], op=ALU.add)
+        gtiles = []
+        for ii in GROWS:
+            pg = gpool.tile([P, C + 1, P], F32, name="pg")
+            for c in range(C):
+                nc.gpsimd.tensor_scalar(out=pg[:, c, :], in0=mt[:, c, ii + 1:ii + 1 + P],
+                                        scalar1=mt[:, c, ii:ii + 1], scalar2=0.0, op0=ALU.subtract, op1=ALU.max)
+            nc.gpsimd.tensor_scalar(out=pg[:, C, :], in0=nhr[:, ii + 1:ii + 1 + P],
+                                    scalar1=nhr[:, ii:ii + 1], scalar2=0.0, op0=ALU.subtract, op1=ALU.add)
+            gtiles.append(pg)
 
         accall = big.tile([P, NFR, P], F32, name="accall")
         l1s = {}
         ess = {}
         ncol = [0]
+        nsum = [0]
 
         def col_add(ii, src):
             k = ncol[0] % 4
@@ -263,28 +253,30 @@ def tile_minibatchdiscrimination_kernel(tc, x, T, out):
             for fi in FBLK[k]:
                 col_add(FROWS[fi], accall[:, fi, 0:P - 1])
 
-        def gp_exp():
-            for gi in range(NGP):
-                ii = GROWS[gi]
-                nc.scalar.activation(out=gacc[:, gi, :], in_=gacc[:, gi, :], func=ACT.Exp, scale=-2.0,
-                                     bias=nrs[:, ii:ii + 1], accum_out=ownf[:, ii:ii + 1])
+        def bank_exp(kind, b):
+            es = work.tile([P, 4, P], F32, name="es4")
+            nr = len((SBANK, GBANK)[kind][b])
+            nc.scalar.activation(out=es[:, 0:nr, :], in_=l1s[kind, b][:, 0:nr, :], func=ACT.Exp,
+                                 scale=(-1.0, -2.0)[kind])
+            ess[kind, b] = es
 
-        def gp_cols():
-            for gi in range(NGP):
-                col_add(GROWS[gi], gacc[:, gi, 0:P - 1])
-
-        def bank_exp(b):
-            ess[b] = work.tile([P, 4, P], F32, name="es4")
-            nr = len(PEBANK[b])
-            nc.scalar.activation(out=ess[b][:, 0:nr, :], in_=l1s[b][:, 0:nr, :], func=ACT.Exp, scale=-1.0)
-
-        def bank_sums(b):
-            for r in range(len(PEBANK[b])):
-                ii = PEBANK[b][r]
-                nc.tensor.matmul(out=colps[:, ii + 1:ii + 1 + P], lhsT=ess[b][:, r, :], rhs=ident[:],
-                                 is_transpose=True, start=False, stop=(4 * b + r == NPR - 1))
-                nc.tensor.matmul(out=ownps[:, ii:ii + 1], lhsT=ess[b][:, r, :], rhs=onesm[:],
+        def bank_sums(kind, b):
+            rows = (SBANK, GBANK)[kind][b]
+            for r in range(len(rows)):
+                ii = rows[r]
+                nsum[0] += 1
+                nc.tensor.matmul(out=colps[:, ii + 1:ii + 1 + P], lhsT=ess[kind, b][:, r, :], rhs=ident[:],
+                                 is_transpose=True, start=False, stop=(nsum[0] == NSC + NGP))
+                nc.tensor.matmul(out=ownps[:, ii:ii + 1], lhsT=ess[kind, b][:, r, :], rhs=onesm[:],
                                  start=True, stop=True)
+
+        def g_add(n):
+            g, c = n // (C + 1), n % (C + 1)
+            b, r = g // 4, g % 4
+            if c == 0 and r == 0:
+                l1s[1, b] = bank(2 + b % 2, [P, 4, P], "l1t")
+            nc.tensor.matmul(out=l1s[1, b][:, r, :], lhsT=gtiles[g][:, c, :], rhs=ident[:], is_transpose=True,
+                             start=(c == 0), stop=(c == C))
 
         steps = []
         for rho in range(C // 2):
@@ -295,7 +287,7 @@ def tile_minibatchdiscrimination_kernel(tc, x, T, out):
         nstt = len(steps)
 
         def slot_of(i):
-            return ((i + 1) * NPR + nstt - 1) // nstt - 1
+            return ((i + 1) * NSC + nstt - 1) // nstt - 1
 
         ev_s = {}
         ev_pe = {}
@@ -304,53 +296,66 @@ def tile_minibatchdiscrimination_kernel(tc, x, T, out):
         def at(table, slot, what):
             table[slot] = table.get(slot, []) + [what]
 
-        for b in range(len(PEBANK)):
-            es_slot = min(4 * b + 3 + LAG, NPR if b == len(PEBANK) - 1 else NPR - 1)
+        NG_PL = NGP * (C + 1)
+
+        def g_upto(n):
+            return min(NG_PL, max(0, n * NG_PL // (NSC * C) - (C + 1)))
+
+        for b in range(len(SBANK)):
+            es_slot = min(4 * b + 3 + LAG, NSC if b == len(SBANK) - 1 else NSC - 1)
             at(ev_s, es_slot, (0, b))
             at(ev_pe, es_slot + 1, (0, b))
+        for b in range(len(GBANK)):
+            nend = (4 * b + len(GBANK[b])) * (C + 1)
+            slot = 0
+            while slot < NSC and g_upto((slot + 1) * C) < nend:
+                slot += 1
+            at(ev_s, slot + 1, (3, b))
+            at(ev_pe, slot + 2, (3, b))
         for rho in range(2, C // 2):
             at(ev_pe, slot_of(int((rho - 0.6) * 2 * NFR)), (1, rho))
-        at(ev_s, NPR - 2, (2, 0))
-        at(ev_v, NPR + 2, (2, 0))
         done = (C // 2 - 1) * 2 * NFR
         for k in range(nblk):
             done += 2 * len(FBLK[k])
             at(ev_s, slot_of(done - 1) + 1, (1, k))
-            at(ev_v, max(slot_of(done - 1) + 2, NPR), (1, k))
+            at(ev_v, max(slot_of(done - 1) + 2, NSC), (1, k))
 
-        for slot in range(NPR + 3):
-            if slot < NPR:
-                for i in range(slot * nstt // NPR, (slot + 1) * nstt // NPR):
+        gdone = 0
+        for slot in range(NSC + 4):
+            if slot < NSC:
+                for i in range(slot * nstt // NSC, (slot + 1) * nstt // NSC):
                     fused_step(steps[i][0], steps[i][1])
             for kind, k in ev_v.get(slot, []):
-                if kind == 1:
-                    fused_cols(k)
-                else:
-                    gp_cols()
-            if slot < NPR:
-                ii = PEROWS[slot]
+                fused_cols(k)
+            if slot < NSC:
+                ii = SROWS[slot]
                 b = slot // 4
                 r = slot % 4
                 if r == 0:
-                    l1s[b] = bank(b % 4, [P, 4, P], "l1t")
+                    l1s[0, b] = bank(b % 2, [P, 4, P], "l1t")
                 pas = aspool.tile([P, C, P], F32, name="pas")
                 for c in range(C):
                     nc.scalar.activation(out=pas[:, c, :], in_=mt[:, c, ii + 1:ii + 1 + P], func=ACT.Abs,
                                          scale=-1.0, bias=mt[:, c, ii:ii + 1])
-                    nc.tensor.matmul(out=l1s[b][:, r, :], lhsT=pas[:, c, :], rhs=ident[:], is_transpose=True,
+                    nc.tensor.matmul(out=l1s[0, b][:, r, :], lhsT=pas[:, c, :], rhs=ident[:], is_transpose=True,
                                      start=(c == 0), stop=(c == C - 1))
+                    while gdone < g_upto(slot * C + c + 1):
+                        g_add(gdone)
+                        gdone += 1
+            else:
+                while gdone < NG_PL:
+                    g_add(gdone)
+                    gdone += 1
             for kind, k in ev_pe.get(slot, []):
-                if kind == 0:
-                    bank_sums(k)
-                else:
+                if kind == 1:
                     load_planes(k)
+                else:
+                    bank_sums(kind // 3, k)
             for kind, k in sorted(ev_s.get(slot, []), key=lambda e: (e[0] == 0, e[0], e[1])):
-                if kind == 0:
-                    bank_exp(k)
-                elif kind == 1:
+                if kind == 1:
                     fused_exp(k)
                 else:
-                    gp_exp()
+                    bank_exp(kind // 3, k)
 
         nc.vector.tensor_tensor(out=w[:], in0=colv[:, 0, :], in1=colps[:], op=ALU.add)
         nc.vector.tensor_tensor(out=colv[:, 1, :], in0=colv[:, 1, :], in1=colv[:, 2, :], op=ALU.add)

@@ -19,8 +19,9 @@ P = 128
 BC = B * C
 FLOPS = 2 * N * A * BC + 3 * N * N * BC
 
-NSC = 48
-NGP = 26
+NSC = 50
+NGP = 20
+WARM = 16
 LAG = 2
 
 
@@ -53,12 +54,14 @@ def tile_minibatchdiscrimination_kernel(tc, x, T, out):
         colv = const.tile([P, 4, 256], F32, name="colv")
         nc.vector.memset(colv[:], 0.0)
         onesm = const.tile([P, 1], F32, name="onesm")
-        mt = const.tile([P, C, 256], F32, name="mt")
-        nhr = const.tile([P, 256], F32, name="nhr")
+        mt = const.tile([P, C + 1, 256], F32, name="mt")
+        nhr = mt[:, C, :]
         rsb = const.tile([P, P], F32, name="rsb")
         u3 = const.tile([P, C, 3, B], F32, name="u3")
         ownf = const.tile([P, P], F32, name="ownf")
         planes = {}
+        xq = const.tile([P, 4, N], U32, name="xq", align_bytes=64)
+        xs = const.tile([P, 4, N], U8, name="xs", align_bytes=64)
         nc.vector.memset(ownf[:], 0.0)
         w = const.tile([P, 256], F32, name="w")
         z1 = const.tile([P, P], F32, name="z1")
@@ -90,8 +93,6 @@ def tile_minibatchdiscrimination_kernel(tc, x, T, out):
                                     op0=ALU.mult, op1=ALU.add)
 
             gx = keep.tile([P, 4, 1024], BF16, name="gx", align_bytes=64)
-            xq = keep.tile([P, 4, N], U32, name="xq", align_bytes=64)
-            xs = keep.tile([P, 4, N], U8, name="xs", align_bytes=64)
             xts = []
             for g in range(4):
                 xt = bank(g, [P, 2, N], "xt")
@@ -189,17 +190,33 @@ def tile_minibatchdiscrimination_kernel(tc, x, T, out):
                     rflat = r3[:].rearrange("p s b -> p (s b)")
                     for u in range(2):
                         nc.tensor.transpose(rps[:, u, :], rflat[:, u * B:u * B + P], ident[:])
-                    nc.vector.tensor_scalar(out=nhr[:], in0=rps[:].rearrange("p u k -> p (u k)"), scalar1=-0.5,
+                    nc.vector.tensor_scalar(out=nhr, in0=rps[:].rearrange("p u k -> p (u k)"), scalar1=-0.5,
                                             scalar2=None, op0=ALU.mult)
                     nc.vector.tensor_copy(out=rsb[:], in_=rps[:, 0, :])
 
-        aspool = ctx.enter_context(tc.tile_pool(name="aspool", bufs=4))
-        gpool = ctx.enter_context(tc.tile_pool(name="gpool", bufs=3))
+        aspool = ctx.enter_context(tc.tile_pool(name="aspool", bufs=3))
+        gpool = ctx.enter_context(tc.tile_pool(name="gpool", bufs=4))
         work = ctx.enter_context(tc.tile_pool(name="work", bufs=4))
         big = ctx.enter_context(tc.tile_pool(name="big", bufs=1))
 
         colps = bank(6, [P, 256], "colps")
-        ownps = bank(7, [P, P], "ownps")
+        own2 = bank(7, [P, 512], "own2")
+        ownps = own2[:, 0:P]
+        ntr = [0]
+
+        def keep_warm():
+            ntr[0] += 1
+            if ntr[0] % WARM == 0:
+                for h in range(2):
+                    nc.tensor.matmul_mx(
+                        out=own2[:, 256:512],
+                        lhsT=xq[:, h, 0:P].bitcast(FP8X4),
+                        lhsT_scale=xs[:, h, 0:P],
+                        rhs=xq[:, 2 + h, :].bitcast(FP8X4),
+                        rhs_scale=xs[:, 2 + h, :],
+                        start=True,
+                        stop=True,
+                    )
 
         def load_planes(rho):
             pl = bank(4 + rho % 2, [P, 2, 256], "pl")
@@ -212,17 +229,23 @@ def tile_minibatchdiscrimination_kernel(tc, x, T, out):
         nc.tensor.matmul(out=colps[:, 0:P], lhsT=zt[:], rhs=ident[:], is_transpose=True, start=True, stop=False)
         nc.tensor.matmul(out=colps[:, P:2 * P], lhsT=zt[:], rhs=ident[:], is_transpose=True, start=False,
                          stop=False)
-        nc.tensor.matmul(out=ownps[:], lhsT=zt[:], rhs=ident[:], is_transpose=True, start=True, stop=True)
+        nc.tensor.matmul(out=ownps, lhsT=zt[:], rhs=ident[:], is_transpose=True, start=True, stop=True)
 
         gtiles = []
-        for ii in GROWS:
+
+        def g_relu(g):
+            nc.gpsimd.tensor_scalar(out=gtiles[g][:, 0:C, :], in0=gtiles[g][:, 0:C, :], scalar1=3.0e38, scalar2=0.0,
+                                    op0=ALU.min, op1=ALU.max)
+
+        for g in range(NGP):
+            ii = GROWS[g]
             pg = gpool.tile([P, C + 1, P], F32, name="pg")
-            for c in range(C):
-                nc.gpsimd.tensor_scalar(out=pg[:, c, :], in0=mt[:, c, ii + 1:ii + 1 + P],
-                                        scalar1=mt[:, c, ii:ii + 1], scalar2=0.0, op0=ALU.subtract, op1=ALU.max)
-            nc.gpsimd.tensor_scalar(out=pg[:, C, :], in0=nhr[:, ii + 1:ii + 1 + P],
-                                    scalar1=nhr[:, ii:ii + 1], scalar2=0.0, op0=ALU.subtract, op1=ALU.add)
+            nc.gpsimd.tensor_tensor(out=pg[:], in0=mt[:, :, ii + 1:ii + 1 + P],
+                                    in1=mt[:, :, ii:ii + 1].to_broadcast([P, C + 1, P]), op=ALU.subtract)
             gtiles.append(pg)
+            if g > 0:
+                g_relu(g - 1)
+        g_relu(NGP - 1)
 
         accall = big.tile([P, NFR, P], F32, name="accall")
         l1s = {}
@@ -277,6 +300,7 @@ def tile_minibatchdiscrimination_kernel(tc, x, T, out):
                 l1s[1, b] = bank(2 + b % 2, [P, 4, P], "l1t")
             nc.tensor.matmul(out=l1s[1, b][:, r, :], lhsT=gtiles[g][:, c, :], rhs=ident[:], is_transpose=True,
                              start=(c == 0), stop=(c == C))
+            keep_warm()
 
         steps = []
         for rho in range(C // 2):
@@ -299,7 +323,7 @@ def tile_minibatchdiscrimination_kernel(tc, x, T, out):
         NG_PL = NGP * (C + 1)
 
         def g_upto(n):
-            return min(NG_PL, max(0, n * NG_PL // (NSC * C) - (C + 1)))
+            return min(NG_PL, max(0, n * NG_PL // (NSC * C) - 2 * (C + 1)))
 
         for b in range(len(SBANK)):
             es_slot = min(4 * b + 3 + LAG, NSC if b == len(SBANK) - 1 else NSC - 1)
@@ -339,6 +363,7 @@ def tile_minibatchdiscrimination_kernel(tc, x, T, out):
                                          scale=-1.0, bias=mt[:, c, ii:ii + 1])
                     nc.tensor.matmul(out=l1s[0, b][:, r, :], lhsT=pas[:, c, :], rhs=ident[:], is_transpose=True,
                                      start=(c == 0), stop=(c == C - 1))
+                    keep_warm()
                     while gdone < g_upto(slot * C + c + 1):
                         g_add(gdone)
                         gdone += 1
@@ -359,7 +384,7 @@ def tile_minibatchdiscrimination_kernel(tc, x, T, out):
 
         nc.vector.tensor_tensor(out=w[:], in0=colv[:, 0, :], in1=colps[:], op=ALU.add)
         nc.vector.tensor_tensor(out=colv[:, 1, :], in0=colv[:, 1, :], in1=colv[:, 2, :], op=ALU.add)
-        nc.vector.tensor_tensor(out=colv[:, 3, 0:P], in0=colv[:, 3, 0:P], in1=ownps[:], op=ALU.add)
+        nc.vector.tensor_tensor(out=colv[:, 3, 0:P], in0=colv[:, 3, 0:P], in1=ownps, op=ALU.add)
         nc.vector.tensor_tensor(out=w[:, 0:P], in0=w[:, 0:P], in1=ownf[:], op=ALU.add)
         nc.vector.tensor_tensor(out=colv[:, 1, :], in0=colv[:, 1, :], in1=colv[:, 3, :], op=ALU.add)
         nc.vector.tensor_tensor(out=w[:], in0=w[:], in1=colv[:, 1, :], op=ALU.add)

@@ -21,7 +21,7 @@ FLOPS = 2 * N * A * BC + 3 * N * N * BC
 
 NSC = 50
 NGP = 20
-WARM = 16
+WARM = 48
 LAG = 2
 
 
@@ -207,13 +207,13 @@ def tile_minibatchdiscrimination_kernel(tc, x, T, out):
         def keep_warm():
             ntr[0] += 1
             if ntr[0] % WARM == 0:
-                for h in range(2):
+                for h in range(6):
                     nc.tensor.matmul_mx(
                         out=own2[:, 256:512],
-                        lhsT=xq[:, h, 0:P].bitcast(FP8X4),
-                        lhsT_scale=xs[:, h, 0:P],
-                        rhs=xq[:, 2 + h, :].bitcast(FP8X4),
-                        rhs_scale=xs[:, 2 + h, :],
+                        lhsT=xq[:, h % 2, 0:P].bitcast(FP8X4),
+                        lhsT_scale=xs[:, h % 2, 0:P],
+                        rhs=xq[:, 2 + h % 2, :].bitcast(FP8X4),
+                        rhs_scale=xs[:, 2 + h % 2, :],
                         start=True,
                         stop=True,
                     )

@@ -19,9 +19,10 @@ P = 128
 BC = B * C
 FLOPS = 2 * N * A * BC + 3 * N * N * BC
 
-NSC = 50
+NSC = 51
 NGP = 20
 WARM = 48
+GLAG = 1.0
 LAG = 2
 
 
@@ -59,38 +60,52 @@ def tile_minibatchdiscrimination_kernel(tc, x, T, out):
         rsb = const.tile([P, P], F32, name="rsb")
         u3 = const.tile([P, C, 3, B], F32, name="u3")
         ownf = const.tile([P, P], F32, name="ownf")
+        res0 = const.tile([P, 1], F32, name="res0")
         planes = {}
         xq = const.tile([P, 4, N], U32, name="xq", align_bytes=64)
         xs = const.tile([P, 4, N], U8, name="xs", align_bytes=64)
         nc.vector.memset(ownf[:], 0.0)
+        nc.scalar.activation(out=res0[:], in_=zt[:, 0:1], func=ACT.Exp)
         w = const.tile([P, 256], F32, name="w")
         z1 = const.tile([P, P], F32, name="z1")
         res = const.tile([P, 2, B], F32, name="res")
 
         with ExitStack() as mxs:
             keep = mxs.enter_context(tc.tile_pool(name="keep", bufs=1))
-            rawp = mxs.enter_context(tc.tile_pool(name="rawp", bufs=4))
+            rawp = mxs.enter_context(tc.tile_pool(name="rawp", bufs=8))
             grpp = mxs.enter_context(tc.tile_pool(name="grpp", bufs=4))
             cdp = mxs.enter_context(tc.tile_pool(name="cdp", bufs=4))
 
+            tv = T.rearrange("(g q j) b c -> g q j (b c)", g=4, q=P, j=4)
             xsb = []
             for m in range(2):
                 xm = keep.tile([P, A], BF16, name="xsb%d" % m)
                 nc.sync.dma_start(out=xm[:], in_=x[m * P:(m + 1) * P, :])
                 xsb.append(xm)
-            tv = T.rearrange("(g q j) b c -> g q j (b c)", g=4, q=P, j=4)
             raws = []
             for g in range(4):
-                raw = rawp.tile([P, 4, BC], BF16, name="raw")
                 for u in range(2):
-                    nc.sync.dma_start(
-                        out=raw[:, :, 1024 * u:1024 * (u + 1)],
-                        in_=tv[g, :, :, 1024 * u:1024 * (u + 1)],
-                    )
-                raws.append(raw)
+                    raw = rawp.tile([P, 4, BC // 2], BF16, name="raw")
+                    nc.sync.dma_start(out=raw[:], in_=tv[g, :, :, 1024 * u:1024 * (u + 1)])
+                    raws.append(raw)
 
             nc.vector.tensor_scalar(out=onesm[:], in0=ident[:, P - 1:P], scalar1=-1.0, scalar2=1.0,
                                     op0=ALU.mult, op1=ALU.add)
+
+            acc = [[None] * 4, [None] * 4]
+            grps = {}
+
+            def regroup(j):
+                grp = grpp.tile([P, 512, 4], BF16, name="grp", align_bytes=64)
+                dst = grp[:].rearrange("p (c i) t -> p c t i", i=4)
+                src = raws[j // 2][:, :, j % 2 * 512:(j % 2 + 1) * 512].rearrange("p t (c i) -> p c t i", i=4)
+                if j % 2 == 0:
+                    nc.vector.tensor_copy(out=dst, in_=src)
+                else:
+                    nc.scalar.copy(out=dst, in_=src)
+                grps[j] = grp
+
+            regroup(0)
 
             gx = keep.tile([P, 4, 1024], BF16, name="gx", align_bytes=64)
             xts = []
@@ -104,26 +119,9 @@ def tile_minibatchdiscrimination_kernel(tc, x, T, out):
             for g in range(4):
                 dst = gx[:, g, :].bitcast(F32).rearrange("p (i u) -> p i u", u=2)
                 src = xts[g][:].rearrange("p u i -> p i u")
-                if g % 2 == 0:
-                    nc.vector.tensor_copy(out=dst, in_=src)
-                else:
-                    nc.scalar.copy(out=dst, in_=src)
+                nc.scalar.copy(out=dst, in_=src)
             for g in range(4):
                 nc.vector.quantize_mx(out=xq[:, g, :].bitcast(FP8X4), scales=xs[:, g, :], in_=gx[:, g, :])
-
-            acc = [[None] * 4, [None] * 4]
-            grps = {}
-
-            def regroup(j):
-                g, nt = j // 4, j % 4
-                grp = grpp.tile([P, 512, 4], BF16, name="grp", align_bytes=64)
-                dst = grp[:].rearrange("p (c i) t -> p c t i", i=4)
-                src = raws[g][:, :, nt * 512:(nt + 1) * 512].rearrange("p t (c i) -> p c t i", i=4)
-                if j % 2 == 0:
-                    nc.vector.tensor_copy(out=dst, in_=src)
-                else:
-                    nc.scalar.copy(out=dst, in_=src)
-                grps[j] = grp
 
             def quant_mm(j):
                 g, nt = j // 4, j % 4
@@ -144,7 +142,6 @@ def tile_minibatchdiscrimination_kernel(tc, x, T, out):
                         stop=(g == 3),
                     )
 
-            regroup(0)
             regroup(1)
             for pr in range(8):
                 if pr < 7:
@@ -162,18 +159,21 @@ def tile_minibatchdiscrimination_kernel(tc, x, T, out):
                 else:
                     nc.scalar.copy(out=dst, in_=src)
 
-            for nt in range(3):
+            evac(1, 0, 1, 1)
+            evac(0, 0, 0, 1)
+            for nt in range(1, 4):
                 evac(0, nt, 0, 0)
-                evac(0, nt, 2, 0)
-            evac(0, 3, 0, 1)
-            evac(0, 3, 2, 1)
-            for nt in range(4):
                 evac(1, nt, 1, 1)
+            nc.vector.tensor_copy(out=u3[:, :, 2, :], in_=u3[:, :, 0, :])
 
+            rv = keep.tile([P, 2, B], F32, name="rv")
+            rt = keep.tile([P, C // 4, 2, B], F32, name="rt")
             r3 = keep.tile([P, 3, B], F32, name="r3")
-            nc.vector.tensor_reduce(out=r3[:, 0:2, :], in_=u3[:, :, 0:2, :].rearrange("p c s b -> p s b c"),
+            nc.gpsimd.tensor_tensor(out=rt[:], in0=u3[:, 16:24, 0:2, :], in1=u3[:, 24:32, 0:2, :], op=ALU.add)
+            for wd in (4, 2, 1):
+                nc.gpsimd.tensor_tensor(out=rt[:, 0:wd], in0=rt[:, 0:wd], in1=rt[:, wd:2 * wd], op=ALU.add)
+            nc.vector.tensor_reduce(out=rv[:], in_=u3[:, 0:16, 0:2, :].rearrange("p c s b -> p s b c"),
                                     axis=mybir.AxisListType.X, op=ALU.add)
-            nc.vector.tensor_copy(out=r3[:, 2, :], in_=r3[:, 0, :])
 
             rps = bank(6, [P, 2, P], "rps")
             for cp in range(C // 2):
@@ -185,14 +185,18 @@ def tile_minibatchdiscrimination_kernel(tc, x, T, out):
                     flat = u3[:, c, :, :].rearrange("p s b -> p (s b)")
                     for u in range(2):
                         nc.tensor.transpose(mtp[:, cc, u * P:(u + 1) * P], flat[:, u * B:u * B + P], ident[:])
-                nc.scalar.copy(out=mt[:, 2 * cp:2 * cp + 2, :], in_=mtp[:])
-                if cp == 11:
-                    rflat = r3[:].rearrange("p s b -> p (s b)")
-                    for u in range(2):
-                        nc.tensor.transpose(rps[:, u, :], rflat[:, u * B:u * B + P], ident[:])
-                    nc.vector.tensor_scalar(out=nhr, in0=rps[:].rearrange("p u k -> p (u k)"), scalar1=-0.5,
-                                            scalar2=None, op0=ALU.mult)
-                    nc.vector.tensor_copy(out=rsb[:], in_=rps[:, 0, :])
+                if cp < 4 or cp % 2 == 1:
+                    nc.scalar.copy(out=mt[:, 2 * cp:2 * cp + 2, :], in_=mtp[:])
+                else:
+                    nc.vector.tensor_copy(out=mt[:, 2 * cp:2 * cp + 2, :], in_=mtp[:])
+            nc.vector.tensor_tensor(out=r3[:, 0:2, :], in0=rv[:], in1=rt[:, 0], op=ALU.add)
+            nc.vector.tensor_tensor(out=r3[:, 2, :], in0=rv[:, 0], in1=rt[:, 0, 0], op=ALU.add)
+            rflat = r3[:].rearrange("p s b -> p (s b)")
+            for u in range(2):
+                nc.tensor.transpose(rps[:, u, :], rflat[:, u * B:u * B + P], ident[:])
+            nc.vector.tensor_scalar(out=nhr, in0=rps[:].rearrange("p u k -> p (u k)"), scalar1=-0.5,
+                                    scalar2=None, op0=ALU.mult)
+            nc.vector.tensor_copy(out=rsb[:], in_=rps[:, 0, :])
 
         aspool = ctx.enter_context(tc.tile_pool(name="aspool", bufs=3))
         gpool = ctx.enter_context(tc.tile_pool(name="gpool", bufs=4))
@@ -232,20 +236,18 @@ def tile_minibatchdiscrimination_kernel(tc, x, T, out):
         nc.tensor.matmul(out=ownps, lhsT=zt[:], rhs=ident[:], is_transpose=True, start=True, stop=True)
 
         gtiles = []
-
-        def g_relu(g):
-            nc.gpsimd.tensor_scalar(out=gtiles[g][:, 0:C, :], in0=gtiles[g][:, 0:C, :], scalar1=3.0e38, scalar2=0.0,
-                                    op0=ALU.min, op1=ALU.max)
-
+        halves = [(0, 17), (17, C + 1)]
         for g in range(NGP):
             ii = GROWS[g]
             pg = gpool.tile([P, C + 1, P], F32, name="pg")
-            nc.gpsimd.tensor_tensor(out=pg[:], in0=mt[:, :, ii + 1:ii + 1 + P],
-                                    in1=mt[:, :, ii:ii + 1].to_broadcast([P, C + 1, P]), op=ALU.subtract)
+            for lo, hi in halves:
+                nc.gpsimd.tensor_tensor(out=pg[:, lo:hi, :], in0=mt[:, lo:hi, ii + 1:ii + 1 + P],
+                                        in1=mt[:, lo:hi, ii:ii + 1].to_broadcast([P, hi - lo, P]), op=ALU.subtract)
+            for lo, hi in halves:
+                hi = min(hi, C)
+                nc.gpsimd.tensor_scalar(out=pg[:, lo:hi, :], in0=pg[:, lo:hi, :], scalar1=3.0e38, scalar2=0.0,
+                                        op0=ALU.min, op1=ALU.max)
             gtiles.append(pg)
-            if g > 0:
-                g_relu(g - 1)
-        g_relu(NGP - 1)
 
         accall = big.tile([P, NFR, P], F32, name="accall")
         l1s = {}
@@ -321,9 +323,10 @@ def tile_minibatchdiscrimination_kernel(tc, x, T, out):
             table[slot] = table.get(slot, []) + [what]
 
         NG_PL = NGP * (C + 1)
+        gdue = [((g + 1) * NSC / (NGP + 1) + GLAG + 2 * c / (C + 1)) * C for g in range(NGP) for c in range(C + 1)]
 
         def g_upto(n):
-            return min(NG_PL, max(0, n * NG_PL // (NSC * C) - 2 * (C + 1)))
+            return sum(1 for due in gdue if due <= n)
 
         for b in range(len(SBANK)):
             es_slot = min(4 * b + 3 + LAG, NSC if b == len(SBANK) - 1 else NSC - 1)
@@ -352,11 +355,11 @@ def tile_minibatchdiscrimination_kernel(tc, x, T, out):
             for kind, k in ev_v.get(slot, []):
                 fused_cols(k)
             if slot < NSC:
-                ii = SROWS[slot]
                 b = slot // 4
                 r = slot % 4
                 if r == 0:
                     l1s[0, b] = bank(b % 2, [P, 4, P], "l1t")
+                ii = SROWS[slot]
                 pas = aspool.tile([P, C, P], F32, name="pas")
                 for c in range(C):
                     nc.scalar.activation(out=pas[:, c, :], in_=mt[:, c, ii + 1:ii + 1 + P], func=ACT.Abs,

@@ -19,8 +19,14 @@ P = 128
 BC = B * C
 FLOPS = 2 * N * A * BC + 3 * N * N * BC
 
-NSC = 51
-NGP = 20
+NSC = 53
+TREE = 6
+HEADMX = 8
+HEADM2 = 4
+HEADCP = (4,)
+BURST = 5
+LOAD = 0.75
+NGP = 17
 WARM = 48
 GLAG = 1.0
 LAG = 2
@@ -70,6 +76,18 @@ def tile_minibatchdiscrimination_kernel(tc, x, T, out):
         z1 = const.tile([P, P], F32, name="z1")
         res = const.tile([P, 2, B], F32, name="res")
 
+        def idle_mx(to, passes):
+            for h in range(passes):
+                nc.tensor.matmul_mx(
+                    out=to,
+                    lhsT=xq[:, h % 2, 0:P].bitcast(FP8X4),
+                    lhsT_scale=xs[:, h % 2, 0:P],
+                    rhs=xq[:, 2 + h % 2, :].bitcast(FP8X4),
+                    rhs_scale=xs[:, 2 + h % 2, :],
+                    start=True,
+                    stop=True,
+                )
+
         with ExitStack() as mxs:
             keep = mxs.enter_context(tc.tile_pool(name="keep", bufs=1))
             rawp = mxs.enter_context(tc.tile_pool(name="rawp", bufs=8))
@@ -105,7 +123,7 @@ def tile_minibatchdiscrimination_kernel(tc, x, T, out):
                     nc.scalar.copy(out=dst, in_=src)
                 grps[j] = grp
 
-            regroup(0)
+            regroup(1)
 
             gx = keep.tile([P, 4, 1024], BF16, name="gx", align_bytes=64)
             xts = []
@@ -119,7 +137,12 @@ def tile_minibatchdiscrimination_kernel(tc, x, T, out):
             for g in range(4):
                 dst = gx[:, g, :].bitcast(F32).rearrange("p (i u) -> p i u", u=2)
                 src = xts[g][:].rearrange("p u i -> p i u")
-                nc.scalar.copy(out=dst, in_=src)
+                if g < 2:
+                    nc.vector.tensor_copy(out=dst, in_=src)
+                else:
+                    nc.scalar.copy(out=dst, in_=src)
+            regroup(0)
+            regroup(2)
             for g in range(4):
                 nc.vector.quantize_mx(out=xq[:, g, :].bitcast(FP8X4), scales=xs[:, g, :], in_=gx[:, g, :])
 
@@ -142,10 +165,10 @@ def tile_minibatchdiscrimination_kernel(tc, x, T, out):
                         stop=(g == 3),
                     )
 
-            regroup(1)
             for pr in range(8):
                 if pr < 7:
-                    regroup(2 * pr + 2)
+                    if pr > 0:
+                        regroup(2 * pr + 2)
                     regroup(2 * pr + 3)
                 quant_mm(2 * pr)
                 quant_mm(2 * pr + 1)
@@ -164,7 +187,10 @@ def tile_minibatchdiscrimination_kernel(tc, x, T, out):
             for nt in range(1, 4):
                 evac(0, nt, 0, 0)
                 evac(1, nt, 1, 1)
-            nc.vector.tensor_copy(out=u3[:, :, 2, :], in_=u3[:, :, 0, :])
+            for c0 in (0, 16):
+                nc.vector.tensor_copy(out=u3[:, c0:c0 + 16, 2, :], in_=u3[:, c0:c0 + 16, 0, :])
+
+            idle_mx(bank(0, [P, 256], "idle")[:], HEADMX)
 
             rv = keep.tile([P, 2, B], F32, name="rv")
             rt = keep.tile([P, C // 4, 2, B], F32, name="rt")
@@ -177,6 +203,8 @@ def tile_minibatchdiscrimination_kernel(tc, x, T, out):
 
             rps = bank(6, [P, 2, P], "rps")
             for cp in range(C // 2):
+                if cp in HEADCP:
+                    idle_mx(bank(7, [P, 256], "idle")[:], HEADM2)
                 mtp = bank(4 + cp if cp < 2 else cp % 4, [P, 2, 256], "mtp")
                 if cp < 2:
                     planes[cp] = mtp
@@ -211,16 +239,7 @@ def tile_minibatchdiscrimination_kernel(tc, x, T, out):
         def keep_warm():
             ntr[0] += 1
             if ntr[0] % WARM == 0:
-                for h in range(6):
-                    nc.tensor.matmul_mx(
-                        out=own2[:, 256:512],
-                        lhsT=xq[:, h % 2, 0:P].bitcast(FP8X4),
-                        lhsT_scale=xs[:, h % 2, 0:P],
-                        rhs=xq[:, 2 + h % 2, :].bitcast(FP8X4),
-                        rhs_scale=xs[:, 2 + h % 2, :],
-                        start=True,
-                        stop=True,
-                    )
+                idle_mx(own2[:, 256:512], BURST)
 
         def load_planes(rho):
             pl = bank(4 + rho % 2, [P, 2, 256], "pl")
@@ -236,6 +255,9 @@ def tile_minibatchdiscrimination_kernel(tc, x, T, out):
         nc.tensor.matmul(out=ownps, lhsT=zt[:], rhs=ident[:], is_transpose=True, start=True, stop=True)
 
         gtiles = []
+        tree = [g for g in range(NGP) if g * TREE // NGP != (g + 1) * TREE // NGP]
+        gplanes = [list(range(C // 2 if g in tree else C)) + [C] for g in range(NGP)]
+        gitems = [(g, c) for g in range(NGP) for c in gplanes[g]]
         halves = [(0, 17), (17, C + 1)]
         for g in range(NGP):
             ii = GROWS[g]
@@ -247,6 +269,9 @@ def tile_minibatchdiscrimination_kernel(tc, x, T, out):
                 hi = min(hi, C)
                 nc.gpsimd.tensor_scalar(out=pg[:, lo:hi, :], in0=pg[:, lo:hi, :], scalar1=3.0e38, scalar2=0.0,
                                         op0=ALU.min, op1=ALU.max)
+            if g in tree:
+                nc.gpsimd.tensor_tensor(out=pg[:, 0:C // 2, :], in0=pg[:, 0:C // 2, :], in1=pg[:, C // 2:C, :],
+                                        op=ALU.add)
             gtiles.append(pg)
 
         accall = big.tile([P, NFR, P], F32, name="accall")
@@ -296,7 +321,7 @@ def tile_minibatchdiscrimination_kernel(tc, x, T, out):
                                  start=True, stop=True)
 
         def g_add(n):
-            g, c = n // (C + 1), n % (C + 1)
+            g, c = gitems[n]
             b, r = g // 4, g % 4
             if c == 0 and r == 0:
                 l1s[1, b] = bank(2 + b % 2, [P, 4, P], "l1t")
@@ -322,8 +347,10 @@ def tile_minibatchdiscrimination_kernel(tc, x, T, out):
         def at(table, slot, what):
             table[slot] = table.get(slot, []) + [what]
 
-        NG_PL = NGP * (C + 1)
-        gdue = [((g + 1) * NSC / (NGP + 1) + GLAG + 2 * c / (C + 1)) * C for g in range(NGP) for c in range(C + 1)]
+        NG_PL = len(gitems)
+        gcost = [1.3 if g in tree else 1.0 for g in range(NGP)]
+        gend = [sum(gcost[:g + 1]) * NSC / (sum(gcost) + 1) for g in range(NGP)]
+        gdue = [(gend[g] + GLAG + 2 * gplanes[g].index(c) / len(gplanes[g])) * C for g, c in gitems]
 
         def g_upto(n):
             return sum(1 for due in gdue if due <= n)
@@ -333,14 +360,14 @@ def tile_minibatchdiscrimination_kernel(tc, x, T, out):
             at(ev_s, es_slot, (0, b))
             at(ev_pe, es_slot + 1, (0, b))
         for b in range(len(GBANK)):
-            nend = (4 * b + len(GBANK[b])) * (C + 1)
+            nend = sum(len(gplanes[g]) for g in range(4 * b + len(GBANK[b])))
             slot = 0
             while slot < NSC and g_upto((slot + 1) * C) < nend:
                 slot += 1
             at(ev_s, slot + 1, (3, b))
             at(ev_pe, slot + 2, (3, b))
         for rho in range(2, C // 2):
-            at(ev_pe, slot_of(int((rho - 0.6) * 2 * NFR)), (1, rho))
+            at(ev_pe, slot_of(int((rho - LOAD) * 2 * NFR)), (1, rho))
         done = (C // 2 - 1) * 2 * NFR
         for k in range(nblk):
             done += 2 * len(FBLK[k])

@@ -20,13 +20,15 @@ BC = B * C
 FLOPS = 2 * N * A * BC + 3 * N * N * BC
 
 NSC = 53
-TREE = 6
+TREE = 4
+VRED = 16
+SFIRST = 4
 HEADMX = 8
 HEADM2 = 4
 HEADCP = (4,)
-BURST = 5
+BURST = 4
 LOAD = 0.75
-NGP = 17
+NGP = 18
 WARM = 48
 GLAG = 1.0
 LAG = 2
@@ -193,13 +195,18 @@ def tile_minibatchdiscrimination_kernel(tc, x, T, out):
             idle_mx(bank(0, [P, 256], "idle")[:], HEADMX)
 
             rv = keep.tile([P, 2, B], F32, name="rv")
-            rt = keep.tile([P, C // 4, 2, B], F32, name="rt")
+            rt = keep.tile([P, (C - VRED) // 2, 2, B], F32, name="rt")
             r3 = keep.tile([P, 3, B], F32, name="r3")
-            nc.gpsimd.tensor_tensor(out=rt[:], in0=u3[:, 16:24, 0:2, :], in1=u3[:, 24:32, 0:2, :], op=ALU.add)
-            for wd in (4, 2, 1):
+            wd = (C - VRED) // 2
+            nc.gpsimd.tensor_tensor(out=rt[:], in0=u3[:, VRED:VRED + wd, 1:3, :], in1=u3[:, VRED + wd:C, 1:3, :],
+                                    op=ALU.add)
+            while wd > 1:
+                wd //= 2
                 nc.gpsimd.tensor_tensor(out=rt[:, 0:wd], in0=rt[:, 0:wd], in1=rt[:, wd:2 * wd], op=ALU.add)
-            nc.vector.tensor_reduce(out=rv[:], in_=u3[:, 0:16, 0:2, :].rearrange("p c s b -> p s b c"),
+            nc.vector.tensor_reduce(out=rv[:], in_=u3[:, 0:VRED, 1:3, :].rearrange("p c s b -> p s b c"),
                                     axis=mybir.AxisListType.X, op=ALU.add)
+            nc.gpsimd.tensor_tensor(out=r3[:, 1:3, :], in0=rv[:], in1=rt[:, 0], op=ALU.add)
+            nc.gpsimd.tensor_tensor(out=r3[:, 0, :], in0=rv[:, 1], in1=rt[:, 0, 1], op=ALU.add)
 
             rps = bank(6, [P, 2, P], "rps")
             for cp in range(C // 2):
@@ -213,12 +220,10 @@ def tile_minibatchdiscrimination_kernel(tc, x, T, out):
                     flat = u3[:, c, :, :].rearrange("p s b -> p (s b)")
                     for u in range(2):
                         nc.tensor.transpose(mtp[:, cc, u * P:(u + 1) * P], flat[:, u * B:u * B + P], ident[:])
-                if cp < 4 or cp % 2 == 1:
+                if cp < SFIRST or cp % 2 == 1:
                     nc.scalar.copy(out=mt[:, 2 * cp:2 * cp + 2, :], in_=mtp[:])
                 else:
                     nc.vector.tensor_copy(out=mt[:, 2 * cp:2 * cp + 2, :], in_=mtp[:])
-            nc.vector.tensor_tensor(out=r3[:, 0:2, :], in0=rv[:], in1=rt[:, 0], op=ALU.add)
-            nc.vector.tensor_tensor(out=r3[:, 2, :], in0=rv[:, 0], in1=rt[:, 0, 0], op=ALU.add)
             rflat = r3[:].rearrange("p s b -> p (s b)")
             for u in range(2):
                 nc.tensor.transpose(rps[:, u, :], rflat[:, u * B:u * B + P], ident[:])
@@ -349,7 +354,7 @@ def tile_minibatchdiscrimination_kernel(tc, x, T, out):
 
         NG_PL = len(gitems)
         gcost = [1.3 if g in tree else 1.0 for g in range(NGP)]
-        gend = [sum(gcost[:g + 1]) * NSC / (sum(gcost) + 1) for g in range(NGP)]
+        gend = [sum(gcost[:g + 1]) * NSC / sum(gcost) for g in range(NGP)]
         gdue = [(gend[g] + GLAG + 2 * gplanes[g].index(c) / len(gplanes[g])) * C for g, c in gitems]
 
         def g_upto(n):

from contextlib import ExitStack

import concourse.mybir as mybir
from concourse.masks import make_identity

FP8X4 = mybir.dt.float8_e4m3fn_x4
F32 = mybir.dt.float32
BF16 = mybir.dt.bfloat16
U32 = mybir.dt.uint32
U8 = mybir.dt.uint8
ALU = mybir.AluOpType
ACT = mybir.ActivationFunctionType

N = 256
A = 2048
B = 64
C = 32
P = 128
BC = B * C
FLOPS = 2 * N * A * BC + 3 * N * N * BC

NSC = 53
TREE = 4
VRED = 16
SFIRST = 4
HEADMX = 8
HEADM2 = 4
HEADCP = (4,)
BURST = 4
LOAD = 0.75
NGP = 18
WARM = 48
GLAG = 1.0
LAG = 2


def tile_minibatchdiscrimination_kernel(tc, x, T, out):
    nc = tc.nc
    quota = [NSC, NGP, P - NSC - NGP]
    owner = []
    for i in range(P):
        owner.append(max(range(3), key=lambda o: quota[o] * (i + 1) - P * sum(1 for w in owner if w == o)))
    SROWS = [i for i in range(P) if owner[i] == 0]
    GROWS = [i for i in range(P) if owner[i] == 1]
    FROWS = [i for i in range(P) if owner[i] == 2]
    NFR = len(FROWS)
    SBANK = [SROWS[4 * k:4 * k + 4] for k in range((NSC + 3) // 4)]
    GBANK = [GROWS[4 * k:4 * k + 4] for k in range((NGP + 3) // 4)]
    nblk = (NFR + 3) // 4
    FBLK = [list(range(k * NFR // nblk, (k + 1) * NFR // nblk)) for k in range(nblk)]
    with ExitStack() as ctx:
        ctx.enter_context(tc.manual_schedule())
        const = ctx.enter_context(tc.tile_pool(name="const", bufs=1))
        psum = ctx.enter_context(tc.psum_pool(name="psum", bufs=1))

        def bank(i, shape, nm):
            return psum.tile(shape, F32, tag="bank%d" % i, name=nm)

        ident = const.tile([P, P], F32, name="ident")
        make_identity(nc, ident[:])
        zt = const.tile([P, P], F32, name="zt")
        nc.vector.memset(zt[:], 0.0)
        colv = const.tile([P, 4, 256], F32, name="colv")
        nc.vector.memset(colv[:], 0.0)
        onesm = const.tile([P, 1], F32, name="onesm")
        mt = const.tile([P, C + 1, 256], F32, name="mt")
        nhr = mt[:, C, :]
        rsb = const.tile([P, P], F32, name="rsb")
        u3 = const.tile([P, C, 3, B], F32, name="u3")
        ownf = const.tile([P, P], F32, name="ownf")
        res0 = const.tile([P, 1], F32, name="res0")
        planes = {}
        xq = const.tile([P, 4, N], U32, name="xq", align_bytes=64)
        xs = const.tile([P, 4, N], U8, name="xs", align_bytes=64)
        nc.vector.memset(ownf[:], 0.0)
        nc.scalar.activation(out=res0[:], in_=zt[:, 0:1], func=ACT.Exp)
        w = const.tile([P, 256], F32, name="w")
        z1 = const.tile([P, P], F32, name="z1")
        res = const.tile([P, 2, B], F32, name="res")

        def idle_mx(to, passes):
            for h in range(passes):
                nc.tensor.matmul_mx(
                    out=to,
                    lhsT=xq[:, h % 2, 0:P].bitcast(FP8X4),
                    lhsT_scale=xs[:, h % 2, 0:P],
                    rhs=xq[:, 2 + h % 2, :].bitcast(FP8X4),
                    rhs_scale=xs[:, 2 + h % 2, :],
                    start=True,
                    stop=True,
                )

        with ExitStack() as mxs:
            keep = mxs.enter_context(tc.tile_pool(name="keep", bufs=1))
            rawp = mxs.enter_context(tc.tile_pool(name="rawp", bufs=8))
            grpp = mxs.enter_context(tc.tile_pool(name="grpp", bufs=4))
            cdp = mxs.enter_context(tc.tile_pool(name="cdp", bufs=4))

            tv = T.rearrange("(g q j) b c -> g q j (b c)", g=4, q=P, j=4)
            xsb = []
            for m in range(2):
                xm = keep.tile([P, A], BF16, name="xsb%d" % m)
                nc.sync.dma_start(out=xm[:], in_=x[m * P:(m + 1) * P, :])
                xsb.append(xm)
            raws = []
            for g in range(4):
                for u in range(2):
                    raw = rawp.tile([P, 4, BC // 2], BF16, name="raw")
                    nc.sync.dma_start(out=raw[:], in_=tv[g, :, :, 1024 * u:1024 * (u + 1)])
                    raws.append(raw)

            nc.vector.tensor_scalar(out=onesm[:], in0=ident[:, P - 1:P], scalar1=-1.0, scalar2=1.0,
                                    op0=ALU.mult, op1=ALU.add)

            acc = [[None] * 4, [None] * 4]
            grps = {}

            def regroup(j):
                grp = grpp.tile([P, 512, 4], BF16, name="grp", align_bytes=64)
                dst = grp[:].rearrange("p (c i) t -> p c t i", i=4)
                src = raws[j // 2][:, :, j % 2 * 512:(j % 2 + 1) * 512].rearrange("p t (c i) -> p c t i", i=4)
                if j % 2 == 0:
                    nc.vector.tensor_copy(out=dst, in_=src)
                else:
                    nc.scalar.copy(out=dst, in_=src)
                grps[j] = grp

            regroup(1)

            gx = keep.tile([P, 4, 1024], BF16, name="gx", align_bytes=64)
            xts = []
            for g in range(4):
                xt = bank(g, [P, 2, N], "xt")
                for m in range(2):
                    for u in range(2):
                        nc.tensor.transpose(xt[:, u, m * P:(m + 1) * P],
                                            xsb[m][:].bitcast(F32)[:, 256 * g + u:256 * (g + 1):2], ident[:])
                xts.append(xt)
            for g in range(4):
                dst = gx[:, g, :].bitcast(F32).rearrange("p (i u) -> p i u", u=2)
                src = xts[g][:].rearrange("p u i -> p i u")
                if g < 2:
                    nc.vector.tensor_copy(out=dst, in_=src)
                else:
                    nc.scalar.copy(out=dst, in_=src)
            regroup(0)
            regroup(2)
            for g in range(4):
                nc.vector.quantize_mx(out=xq[:, g, :].bitcast(FP8X4), scales=xs[:, g, :], in_=gx[:, g, :])

            def quant_mm(j):
                g, nt = j // 4, j % 4
                tq = cdp.tile([P, 512], U32, name="tq", align_bytes=64)
                ts = cdp.tile([P, 512], U8, name="ts", align_bytes=64)
                nc.vector.quantize_mx(out=tq[:].bitcast(FP8X4), scales=ts[:],
                                      in_=grps[j][:].rearrange("p n t -> p (n t)"))
                for m in range(2):
                    if g == 0:
                        acc[m][nt] = bank(4 * m + nt, [P, 512], "acc")
                    nc.tensor.matmul_mx(
                        out=acc[m][nt][:],
                        lhsT=xq[:, g, m * P:(m + 1) * P].bitcast(FP8X4),
                        lhsT_scale=xs[:, g, m * P:(m + 1) * P],
                        rhs=tq[:].bitcast(FP8X4),
                        rhs_scale=ts[:],
                        start=(g == 0),
                        stop=(g == 3),
                    )

            for pr in range(8):
                if pr < 7:
                    if pr > 0:
                        regroup(2 * pr + 2)
                    regroup(2 * pr + 3)
                quant_mm(2 * pr)
                quant_mm(2 * pr + 1)


            def evac(m, nt, s, eng):
                dst = u3[:, :, s, 16 * nt:16 * nt + 16]
                src = acc[m][nt][:].rearrange("p (b c) -> p c b", c=C)
                if eng == 0:
                    nc.vector.tensor_copy(out=dst, in_=src)
                else:
                    nc.scalar.copy(out=dst, in_=src)

            evac(1, 0, 1, 1)
            evac(0, 0, 0, 1)
            for nt in range(1, 4):
                evac(0, nt, 0, 0)
                evac(1, nt, 1, 1)
            for c0 in (0, 16):
                nc.vector.tensor_copy(out=u3[:, c0:c0 + 16, 2, :], in_=u3[:, c0:c0 + 16, 0, :])

            idle_mx(bank(0, [P, 256], "idle")[:], HEADMX)

            rv = keep.tile([P, 2, B], F32, name="rv")
            rt = keep.tile([P, (C - VRED) // 2, 2, B], F32, name="rt")
            r3 = keep.tile([P, 3, B], F32, name="r3")
            wd = (C - VRED) // 2
            nc.gpsimd.tensor_tensor(out=rt[:], in0=u3[:, VRED:VRED + wd, 1:3, :], in1=u3[:, VRED + wd:C, 1:3, :],
                                    op=ALU.add)
            while wd > 1:
                wd //= 2
                nc.gpsimd.tensor_tensor(out=rt[:, 0:wd], in0=rt[:, 0:wd], in1=rt[:, wd:2 * wd], op=ALU.add)
            nc.vector.tensor_reduce(out=rv[:], in_=u3[:, 0:VRED, 1:3, :].rearrange("p c s b -> p s b c"),
                                    axis=mybir.AxisListType.X, op=ALU.add)
            nc.gpsimd.tensor_tensor(out=r3[:, 1:3, :], in0=rv[:], in1=rt[:, 0], op=ALU.add)
            nc.gpsimd.tensor_tensor(out=r3[:, 0, :], in0=rv[:, 1], in1=rt[:, 0, 1], op=ALU.add)

            rps = bank(6, [P, 2, P], "rps")
            for cp in range(C // 2):
                if cp in HEADCP:
                    idle_mx(bank(7, [P, 256], "idle")[:], HEADM2)
                mtp = bank(4 + cp if cp < 2 else cp % 4, [P, 2, 256], "mtp")
                if cp < 2:
                    planes[cp] = mtp
                for cc in range(2):
                    c = 2 * cp + cc
                    flat = u3[:, c, :, :].rearrange("p s b -> p (s b)")
                    for u in range(2):
                        nc.tensor.transpose(mtp[:, cc, u * P:(u + 1) * P], flat[:, u * B:u * B + P], ident[:])
                if cp < SFIRST or cp % 2 == 1:
                    nc.scalar.copy(out=mt[:, 2 * cp:2 * cp + 2, :], in_=mtp[:])
                else:
                    nc.vector.tensor_copy(out=mt[:, 2 * cp:2 * cp + 2, :], in_=mtp[:])
            rflat = r3[:].rearrange("p s b -> p (s b)")
            for u in range(2):
                nc.tensor.transpose(rps[:, u, :], rflat[:, u * B:u * B + P], ident[:])
            nc.vector.tensor_scalar(out=nhr, in0=rps[:].rearrange("p u k -> p (u k)"), scalar1=-0.5,
                                    scalar2=None, op0=ALU.mult)
            nc.vector.tensor_copy(out=rsb[:], in_=rps[:, 0, :])

        aspool = ctx.enter_context(tc.tile_pool(name="aspool", bufs=3))
        gpool = ctx.enter_context(tc.tile_pool(name="gpool", bufs=4))
        work = ctx.enter_context(tc.tile_pool(name="work", bufs=4))
        big = ctx.enter_context(tc.tile_pool(name="big", bufs=1))

        colps = bank(6, [P, 256], "colps")
        own2 = bank(7, [P, 512], "own2")
        ownps = own2[:, 0:P]
        ntr = [0]

        def keep_warm():
            ntr[0] += 1
            if ntr[0] % WARM == 0:
                idle_mx(own2[:, 256:512], BURST)

        def load_planes(rho):
            pl = bank(4 + rho % 2, [P, 2, 256], "pl")
            for cc in range(2):
                flat = u3[:, 2 * rho + cc, :, :].rearrange("p s b -> p (s b)")
                for u in range(2):
                    nc.tensor.transpose(pl[:, cc, u * P:(u + 1) * P], flat[:, u * B:u * B + P], ident[:])
            planes[rho] = pl

        nc.tensor.matmul(out=colps[:, 0:P], lhsT=zt[:], rhs=ident[:], is_transpose=True, start=True, stop=False)
        nc.tensor.matmul(out=colps[:, P:2 * P], lhsT=zt[:], rhs=ident[:], is_transpose=True, start=False,
                         stop=False)
        nc.tensor.matmul(out=ownps, lhsT=zt[:], rhs=ident[:], is_transpose=True, start=True, stop=True)

        gtiles = []
        tree = [g for g in range(NGP) if g * TREE // NGP != (g + 1) * TREE // NGP]
        gplanes = [list(range(C // 2 if g in tree else C)) + [C] for g in range(NGP)]
        gitems = [(g, c) for g in range(NGP) for c in gplanes[g]]
        halves = [(0, 17), (17, C + 1)]
        for g in range(NGP):
            ii = GROWS[g]
            pg = gpool.tile([P, C + 1, P], F32, name="pg")
            for lo, hi in halves:
                nc.gpsimd.tensor_tensor(out=pg[:, lo:hi, :], in0=mt[:, lo:hi, ii + 1:ii + 1 + P],
                                        in1=mt[:, lo:hi, ii:ii + 1].to_broadcast([P, hi - lo, P]), op=ALU.subtract)
            for lo, hi in halves:
                hi = min(hi, C)
                nc.gpsimd.tensor_scalar(out=pg[:, lo:hi, :], in0=pg[:, lo:hi, :], scalar1=3.0e38, scalar2=0.0,
                                        op0=ALU.min, op1=ALU.max)
            if g in tree:
                nc.gpsimd.tensor_tensor(out=pg[:, 0:C // 2, :], in0=pg[:, 0:C // 2, :], in1=pg[:, C // 2:C, :],
                                        op=ALU.add)
            gtiles.append(pg)

        accall = big.tile([P, NFR, P], F32, name="accall")
        l1s = {}
        ess = {}
        ncol = [0]
        nsum = [0]

        def col_add(ii, src):
            k = ncol[0] % 4
            ncol[0] += 1
            nc.vector.tensor_tensor(out=colv[:, k, ii + 1:ii + P], in0=colv[:, k, ii + 1:ii + P], in1=src,
                                    op=ALU.add)

        def fused_step(fi, c):
            ii = FROWS[fi]
            pl = planes[c // 2]
            prev = nhr[:, ii + 1:ii + 1 + P] if c == 0 else accall[:, fi, :]
            nc.vector.scalar_tensor_tensor(out=accall[:, fi, :], in0=pl[:, c % 2, ii + 1:ii + 1 + P],
                                           scalar=pl[:, c % 2, ii:ii + 1], in1=prev, op0=ALU.max, op1=ALU.add)

        def fused_exp(k):
            for fi in FBLK[k]:
                ii = FROWS[fi]
                nc.scalar.activation(out=accall[:, fi, :], in_=accall[:, fi, :], func=ACT.Exp, scale=-2.0,
                                     bias=rsb[:, ii:ii + 1], accum_out=ownf[:, ii:ii + 1])

        def fused_cols(k):
            for fi in FBLK[k]:
                col_add(FROWS[fi], accall[:, fi, 0:P - 1])

        def bank_exp(kind, b):
            es = work.tile([P, 4, P], F32, name="es4")
            nr = len((SBANK, GBANK)[kind][b])
            nc.scalar.activation(out=es[:, 0:nr, :], in_=l1s[kind, b][:, 0:nr, :], func=ACT.Exp,
                                 scale=(-1.0, -2.0)[kind])
            ess[kind, b] = es

        def bank_sums(kind, b):
            rows = (SBANK, GBANK)[kind][b]
            for r in range(len(rows)):
                ii = rows[r]
                nsum[0] += 1
                nc.tensor.matmul(out=colps[:, ii + 1:ii + 1 + P], lhsT=ess[kind, b][:, r, :], rhs=ident[:],
                                 is_transpose=True, start=False, stop=(nsum[0] == NSC + NGP))
                nc.tensor.matmul(out=ownps[:, ii:ii + 1], lhsT=ess[kind, b][:, r, :], rhs=onesm[:],
                                 start=True, stop=True)

        def g_add(n):
            g, c = gitems[n]
            b, r = g // 4, g % 4
            if c == 0 and r == 0:
                l1s[1, b] = bank(2 + b % 2, [P, 4, P], "l1t")
            nc.tensor.matmul(out=l1s[1, b][:, r, :], lhsT=gtiles[g][:, c, :], rhs=ident[:], is_transpose=True,
                             start=(c == 0), stop=(c == C))
            keep_warm()

        steps = []
        for rho in range(C // 2):
            for blk in FBLK:
                for cc in range(2):
                    for fi in blk:
                        steps.append((fi, 2 * rho + cc))
        nstt = len(steps)

        def slot_of(i):
            return ((i + 1) * NSC + nstt - 1) // nstt - 1

        ev_s = {}
        ev_pe = {}
        ev_v = {}

        def at(table, slot, what):
            table[slot] = table.get(slot, []) + [what]

        NG_PL = len(gitems)
        gcost = [1.3 if g in tree else 1.0 for g in range(NGP)]
        gend = [sum(gcost[:g + 1]) * NSC / sum(gcost) for g in range(NGP)]
        gdue = [(gend[g] + GLAG + 2 * gplanes[g].index(c) / len(gplanes[g])) * C for g, c in gitems]

        def g_upto(n):
            return sum(1 for due in gdue if due <= n)

        for b in range(len(SBANK)):
            es_slot = min(4 * b + 3 + LAG, NSC if b == len(SBANK) - 1 else NSC - 1)
            at(ev_s, es_slot, (0, b))
            at(ev_pe, es_slot + 1, (0, b))
        for b in range(len(GBANK)):
            nend = sum(len(gplanes[g]) for g in range(4 * b + len(GBANK[b])))
            slot = 0
            while slot < NSC and g_upto((slot + 1) * C) < nend:
                slot += 1
            at(ev_s, slot + 1, (3, b))
            at(ev_pe, slot + 2, (3, b))
        for rho in range(2, C // 2):
            at(ev_pe, slot_of(int((rho - LOAD) * 2 * NFR)), (1, rho))
        done = (C // 2 - 1) * 2 * NFR
        for k in range(nblk):
            done += 2 * len(FBLK[k])
            at(ev_s, slot_of(done - 1) + 1, (1, k))
            at(ev_v, max(slot_of(done - 1) + 2, NSC), (1, k))

        gdone = 0
        for slot in range(NSC + 4):
            if slot < NSC:
                for i in range(slot * nstt // NSC, (slot + 1) * nstt // NSC):
                    fused_step(steps[i][0], steps[i][1])
            for kind, k in ev_v.get(slot, []):
                fused_cols(k)
            if slot < NSC:
                b = slot // 4
                r = slot % 4
                if r == 0:
                    l1s[0, b] = bank(b % 2, [P, 4, P], "l1t")
                ii = SROWS[slot]
                pas = aspool.tile([P, C, P], F32, name="pas")
                for c in range(C):
                    nc.scalar.activation(out=pas[:, c, :], in_=mt[:, c, ii + 1:ii + 1 + P], func=ACT.Abs,
                                         scale=-1.0, bias=mt[:, c, ii:ii + 1])
                    nc.tensor.matmul(out=l1s[0, b][:, r, :], lhsT=pas[:, c, :], rhs=ident[:], is_transpose=True,
                                     start=(c == 0), stop=(c == C - 1))
                    keep_warm()
                    while gdone < g_upto(slot * C + c + 1):
                        g_add(gdone)
                        gdone += 1
            else:
                while gdone < NG_PL:
                    g_add(gdone)
                    gdone += 1
            for kind, k in ev_pe.get(slot, []):
                if kind == 1:
                    load_planes(k)
                else:
                    bank_sums(kind // 3, k)
            for kind, k in sorted(ev_s.get(slot, []), key=lambda e: (e[0] == 0, e[0], e[1])):
                if kind == 1:
                    fused_exp(k)
                else:
                    bank_exp(kind // 3, k)

        nc.vector.tensor_tensor(out=w[:], in0=colv[:, 0, :], in1=colps[:], op=ALU.add)
        nc.vector.tensor_tensor(out=colv[:, 1, :], in0=colv[:, 1, :], in1=colv[:, 2, :], op=ALU.add)
        nc.vector.tensor_tensor(out=colv[:, 3, 0:P], in0=colv[:, 3, 0:P], in1=ownps, op=ALU.add)
        nc.vector.tensor_tensor(out=w[:, 0:P], in0=w[:, 0:P], in1=ownf[:], op=ALU.add)
        nc.vector.tensor_tensor(out=colv[:, 1, :], in0=colv[:, 1, :], in1=colv[:, 3, :], op=ALU.add)
        nc.vector.tensor_tensor(out=w[:], in0=w[:], in1=colv[:, 1, :], op=ALU.add)
        zps = bank(0, [P, 2, P], "zps")
        for u in range(2):
            nc.tensor.transpose(zps[:, u, :], w[:, u * P:(u + 1) * P], ident[:])
        nc.vector.tensor_copy(out=z1[:], in_=zps[:, 1, :])
        for h in range(2):
            nc.vector.scalar_tensor_tensor(out=res[:, h, :], in0=zps[:, 0, h * B:(h + 1) * B], scalar=1.0,
                                           in1=z1[:, (1 - h) * B:(2 - h) * B], op0=ALU.add, op1=ALU.add)
        nc.sync.dma_start(out=out.rearrange("(h t) b -> t h b", h=2), in_=res[:])
